import numpy as np
import ml_dtypes


def mxq(x, axis, fmt="e4m3"):
    dtype, down = {"e4m3": (ml_dtypes.float8_e4m3fn, 7), "e5m2": (ml_dtypes.float8_e5m2, 14)}[fmt]
    v = np.moveaxis(np.asarray(x, np.float32).astype(ml_dtypes.bfloat16).astype(np.float64), axis, -1)
    blocks = v.reshape(v.shape[:-1] + (-1, 32))
    amax = np.abs(blocks).max(-1, keepdims=True)
    byte = np.maximum(np.where(amax > 0, np.frexp(amax)[1] - 1 + 127, 0) - down, 1)
    scale = np.exp2(byte - 127.0)
    codes = (blocks / scale).astype(np.float32).astype(dtype).astype(np.float64)
    return np.moveaxis((codes * scale).reshape(v.shape), -1, axis)


WIDE = False


def mx_kscale(k):
    if not WIDE:
        return np.ones(k)
    levels = np.array([10, -10, 5, -5, 0])
    a = np.random.permutation(np.resize(levels, k // 512 * 4)).reshape(k // 512, 4)
    idx = np.arange(k)
    return np.exp2(a[idx // 512, idx % 128 // 32])


BF16 = ml_dtypes.bfloat16


def bf(x):
    return np.asarray(x, np.float32).astype(BF16)


def f64(x):
    return np.asarray(x).astype(np.float64)


E2M1 = np.array([0.0, 0.5, 1.0, 1.5, 2.0, 3.0, 4.0, 6.0, -0.0, -0.5, -1.0, -1.5, -2.0, -3.0, -4.0, -6.0])


def pack_weight(w, fmt):
    k, n = w.shape
    w = f64(bf(w)).reshape(k // 32, 32, n)
    amax = np.abs(w).max(1)
    if fmt == "e4m3":
        byte = np.frexp(amax)[1] - 1 + 127 - 7
    else:
        mant, ex = np.frexp(amax / 6.0)
        byte = np.where(mant > 0.5, ex, ex - 1) + 127
    byte = np.clip(np.where(amax > 0, byte, 1), 1, 254)
    scaled = (w * np.exp2(127.0 - byte)[:, None, :]).reshape(k, n).astype(np.float32)
    by_word = np.ascontiguousarray(scaled.reshape(k // 512, 128, 4, n).transpose(0, 1, 3, 2))
    if fmt == "e4m3":
        words = by_word.astype(ml_dtypes.float8_e4m3fn).view(np.uint8)
    else:
        c = by_word.astype(ml_dtypes.float4_e2m1fn).view(np.uint8) & 0xF
        words = c[..., 0::2] | (c[..., 1::2] << 4)
    return np.ascontiguousarray(words), np.ascontiguousarray(byte.astype(np.uint8).reshape(k // 512, 16, n))


def unpack_weight(words, scales, fmt):
    g, p, n, _ = words.shape
    if fmt == "e4m3":
        vals = np.ascontiguousarray(words).view(ml_dtypes.float8_e4m3fn).astype(np.float64)
    else:
        nib = np.empty((g, p, n, 4), np.uint8)
        nib[..., 0::2] = words & 0xF
        nib[..., 1::2] = words >> 4
        vals = E2M1[nib]
    vals = vals * np.repeat(np.exp2(scales.astype(np.float64) - 127.0), 8, axis=1)[..., None]
    return vals.transpose(0, 1, 3, 2).reshape(g * 512, n)


B, D_IN, H = 128, 2048, 1024


def sigmoid(v):
    return 1.0 / (1.0 + np.exp(-v))


def setup_inputs():
    s, u, v = mx_kscale(D_IN), mx_kscale(H), mx_kscale(H)
    one = np.ones(H)
    inp = {"x": bf(np.random.standard_normal((B, D_IN)) * s),
           "hidden_memory_tm1": bf(np.random.standard_normal((B, 2 * H)) * np.concatenate([u, one])),
           "hidden_memory_tm2": bf(np.random.standard_normal((B, 2 * H)) * np.concatenate([v, one]))}
    for g in "ifoc":
        inp["W" + g + "_words"], inp["W" + g + "_scales"] = pack_weight(np.random.standard_normal((D_IN, H)) * 0.6 / np.sqrt(D_IN) / s[:, None], "e4m3")
        inp["U" + g + "_words"], inp["U" + g + "_scales"] = pack_weight(np.random.standard_normal((H, H)) * 0.6 / np.sqrt(H) / u[:, None], "e4m3")
        inp["V" + g + "_words"], inp["V" + g + "_scales"] = pack_weight(np.random.standard_normal((H, H)) * 0.6 / np.sqrt(H) / v[:, None], "e4m3")
    return inp


def reference(x, hidden_memory_tm1, hidden_memory_tm2, Wi_words, Wi_scales, Ui_words, Ui_scales, Vi_words, Vi_scales, Wf_words, Wf_scales, Uf_words, Uf_scales, Vf_words, Vf_scales, Wo_words, Wo_scales, Uo_words, Uo_scales, Vo_words, Vo_scales, Wc_words, Wc_scales, Uc_words, Uc_scales, Vc_words, Vc_scales):
    hm1 = f64(hidden_memory_tm1)
    hm2 = f64(hidden_memory_tm2)
    h_prev = hm1[:, :H]
    c_prev = hm1[:, H:]
    h_cross = hm2[:, :H]
    W = np.concatenate([unpack_weight(Wi_words, Wi_scales, "e4m3"), unpack_weight(Wf_words, Wf_scales, "e4m3"), unpack_weight(Wo_words, Wo_scales, "e4m3"), unpack_weight(Wc_words, Wc_scales, "e4m3")], axis=1)
    U = np.concatenate([unpack_weight(Ui_words, Ui_scales, "e4m3"), unpack_weight(Uf_words, Uf_scales, "e4m3"), unpack_weight(Uo_words, Uo_scales, "e4m3"), unpack_weight(Uc_words, Uc_scales, "e4m3")], axis=1)
    V = np.concatenate([unpack_weight(Vi_words, Vi_scales, "e4m3"), unpack_weight(Vf_words, Vf_scales, "e4m3"), unpack_weight(Vo_words, Vo_scales, "e4m3"), unpack_weight(Vc_words, Vc_scales, "e4m3")], axis=1)
    gates = ((mxq(f64(x), 1, "e4m3") @ W)
             + (mxq(h_prev, 1, "e4m3") @ U)
             + (mxq(h_cross, 1, "e4m3") @ V))
    i = sigmoid(gates[:, 0 * H:1 * H])
    f = sigmoid(gates[:, 1 * H:2 * H])
    o = sigmoid(gates[:, 2 * H:3 * H])
    c_ = np.tanh(gates[:, 3 * H:4 * H])
    c = f * c_prev + i * c_
    h = o * np.tanh(c)
    new_state = np.concatenate([h, c], axis=-1)
    return h, new_state

@@ -1,0 +1,200 @@
+import concourse.mybir as mybir
+from concourse.masks import make_identity
+
+F32 = mybir.dt.float32
+BF16 = mybir.dt.bfloat16
+I32 = mybir.dt.int32
+U32 = mybir.dt.uint32
+U8 = mybir.dt.uint8
+FP8X4 = mybir.dt.float8_e4m3fn_x4
+ACT = mybir.ActivationFunctionType
+ALU = mybir.AluOpType
+
+P = 128
+H = 1024
+FLOPS = 2 * 128 * 4096 * 4096
+BYTES = 20185088
+
+GATE_SLOT = {"i": 0, "f": 1, "o": 2, "c": 3}
+SW_SCALES = True
+
+
+def tile_bilaterallstmcell_w_kernel(tc, x, hm1, hm2, *rest):
+    nc = tc.nc
+    out_h, out_state = rest[24], rest[25]
+
+    def gate_inputs(gate):
+        base = 6 * GATE_SLOT[gate]
+        return rest[base:base + 6]
+
+    with tc.tile_pool(name="keep", bufs=1) as keep, tc.psum_pool(name="psum", bufs=8) as psum, tc.manual_schedule():
+        planes = {}
+        for gate in "fico":
+            for kind in ("w", "uv"):
+                pl = keep.tile([P, H], U8, name="pl_%s_%s" % (kind, gate), align_bytes=64)
+                nc.vector.memset(pl[:].bitcast(I32), 0)
+                planes[(kind, gate)] = pl
+        warm = keep.tile([P, 8], F32, name="warm")
+        warm2 = keep.tile([P, 8], F32, name="warm2")
+        nc.vector.memset(warm[:], 0.0)
+        nc.scalar.activation(out=warm2[:], in_=warm[:], func=ACT.Sigmoid)
+        ident = keep.tile([P, P], F32, name="ident")
+        make_identity(nc, ident[:])
+
+        x_sb = keep.tile([P, 2048], BF16, name="x_sb")
+        hm1_sb = keep.tile([P, 2048], BF16, name="hm1_sb")
+        hc_sb = keep.tile([P, H], BF16, name="hc_sb")
+        nc.sync.dma_start(out=x_sb[:], in_=x)
+        nc.sync.dma_start(out=hm1_sb[:], in_=hm1)
+        nc.sync.dma_start(out=hc_sb[:], in_=hm2[:, 0:H])
+
+        def load_scales(gate, which, hw):
+            ins = gate_inputs(gate)
+            if which == "w":
+                src, pl, first, count = ins[1], planes[("w", gate)], 0, 16
+            elif which == "u":
+                src, pl, first, count = ins[3], planes[("uv", gate)], 0, 8
+            else:
+                src, pl, first, count = ins[5], planes[("uv", gate)], 8, 8
+            for q in range(4):
+                dst = pl[32 * q + first:32 * q + first + count, :]
+                rows = src[:, 4 * q:4 * q + 4, :]
+                if hw:
+                    nc.sync.dma_start(out=dst.bitcast(I32), in_=rows.bitcast(I32))
+                else:
+                    nc.gpsimd.dma_start(out=dst.bitcast(F32), in_=rows.bitcast(F32))
+
+        load_scales("f", "w", True)
+        for gate in "fico":
+            for which in "wuv":
+                if (gate, which) != ("f", "w"):
+                    load_scales(gate, which, not SW_SCALES)
+
+        words = {}
+        for gate in "fico":
+            ins = gate_inputs(gate)
+            w_src = ins[0].rearrange("g p n t -> p g (n t)")
+            u_src = ins[2].rearrange("g p n t -> p g (n t)")
+            v_src = ins[4].rearrange("g p n t -> p g (n t)")
+            for name, src in (("w01", w_src[:, 0:2, :]), ("w23", w_src[:, 2:4, :]), ("u01", u_src)):
+                t = keep.tile([P, 2, H], U32, name="%s_%s" % (name, gate), align_bytes=64)
+                nc.sync.dma_start(out=t[:].bitcast(I32), in_=src.bitcast(I32))
+                words[(name, gate)] = t
+            if gate != "o":
+                t = keep.tile([P, 2, H], U32, name="v01_%s" % gate, align_bytes=64)
+                nc.sync.dma_start(out=t[:].bitcast(I32), in_=v_src.bitcast(I32))
+                words[("v01", gate)] = t
+            else:
+                t = keep.tile([P, H], U32, name="v0_o", align_bytes=64)
+                nc.sync.dma_start(out=t[:].bitcast(I32), in_=v_src[:, 0, :].bitcast(I32))
+                words[("v0", gate)] = t
+                for j in range(4):
+                    t = keep.tile([P, 256], U32, name="v1_o_%d" % j, align_bytes=64)
+                    nc.sync.dma_start(out=t[:].bitcast(I32), in_=v_src[:, 1, 1024 * j:1024 * (j + 1)].bitcast(I32))
+                    words[("v1", j)] = t
+
+        sources = (
+            (x_sb[:].bitcast(F32), 0), (x_sb[:].bitcast(F32), 2),
+            (hm1_sb[:].bitcast(F32), 0), (hc_sb[:].bitcast(F32), 0),
+        )
+        banks = []
+        for b, (src, g0) in enumerate(sources):
+            xt = psum.tile([P, 512], F32, name="xt%d" % b, tag="bank")
+            for gl in range(2):
+                for u in range(2):
+                    g = g0 + gl
+                    nc.tensor.transpose(xt[:, (2 * gl + u) * P:(2 * gl + u + 1) * P], src[:, 256 * g + u:256 * (g + 1):2], ident[:])
+            banks.append(xt)
+        grouped = []
+        for b in (0, 2, 1, 3):
+            gr = keep.tile([P, 1024], BF16, name="grouped%d" % b, align_bytes=64)
+            dst = gr[:].bitcast(F32).rearrange("p (g b u) -> p g b u", g=2, u=2)
+            srcv = banks[b][:].rearrange("p (g u b) -> p g b u", g=2, u=2)
+            if b % 2 == 0:
+                nc.vector.tensor_copy(out=dst, in_=srcv)
+            else:
+                nc.scalar.copy(out=dst, in_=srcv)
+            grouped.append((b, gr))
+        grouped = dict(grouped)
+        a_codes, a_scales = [], []
+        for b in range(4):
+            co = keep.tile([P, 256], U32, name="a_codes%d" % b, align_bytes=64)
+            sc = keep.tile([P, 256], U8, name="a_scales%d" % b, align_bytes=64)
+            nc.vector.quantize_mx(out=co[:].bitcast(FP8X4), scales=sc[:], in_=grouped[b][:])
+            a_codes.append(co)
+            a_scales.append(sc)
+
+        def stationary(k_pass):
+            b, l = k_pass // 2, k_pass % 2
+            return a_codes[b][:, l * P:(l + 1) * P].bitcast(FP8X4), a_scales[b][:, l * P:(l + 1) * P]
+
+        def plane_rows(pl, offset, cols):
+            if offset == 0:
+                return pl[:, cols]
+            return pl[offset:P, cols]
+
+        def moving(gate, k_pass, cols):
+            if k_pass < 4:
+                t = words[("w01" if k_pass < 2 else "w23", gate)]
+                return t[:, k_pass % 2, cols], plane_rows(planes[("w", gate)], 4 * k_pass, cols)
+            pl = plane_rows(planes[("uv", gate)], 4 * (k_pass - 4), cols)
+            if k_pass < 6:
+                return words[("u01", gate)][:, k_pass - 4, cols], pl
+            return words[("v01", gate)][:, k_pass - 6, cols], pl
+
+        def mx(acc, gate, k_pass, cols, rhs=None):
+            lhsT, lhsT_scale = stationary(k_pass)
+            if rhs is None:
+                rhs, rhs_scale = moving(gate, k_pass, cols)
+            else:
+                rhs_scale = plane_rows(planes[("uv", gate)], 4 * (k_pass - 4), cols)
+            nc.tensor.matmul_mx(out=acc[:], lhsT=lhsT, lhsT_scale=lhsT_scale, rhs=rhs.bitcast(FP8X4), rhs_scale=rhs_scale,
+                                start=(k_pass == 0), stop=(k_pass == 7))
+
+        def gate_sums(gate):
+            accs = [psum.tile([P, 512], F32, name="acc_%s%d" % (gate, h), tag="bank") for h in range(2)]
+            for k_pass in range(8):
+                for h in range(2):
+                    mx(accs[h], gate, k_pass, slice(512 * h, 512 * (h + 1)))
+            return accs
+
+        halves = [slice(0, 512), slice(512, 1024)]
+        c_prev = hm1_sb[:, H:2 * H]
+        sf = keep.tile([P, H], F32, name="sf")
+        fc = keep.tile([P, H], F32, name="fc")
+        si = keep.tile([P, H], F32, name="si")
+        tcand = keep.tile([P, H], F32, name="tcand")
+        ic = keep.tile([P, H], F32, name="ic")
+        c_new = keep.tile([P, H], F32, name="c_new")
+        th = keep.tile([P, H], F32, name="th")
+
+        accs = gate_sums("f")
+        for h in range(2):
+            nc.scalar.activation(out=sf[:, halves[h]], in_=accs[h][:], func=ACT.Sigmoid)
+            nc.vector.tensor_tensor(out=fc[:, halves[h]], in0=sf[:, halves[h]], in1=c_prev[:, halves[h]], op=ALU.mult)
+        accs = gate_sums("i")
+        for h in range(2):
+            nc.scalar.activation(out=si[:, halves[h]], in_=accs[h][:], func=ACT.Sigmoid)
+        accs = gate_sums("c")
+        for h in range(2):
+            nc.scalar.activation(out=tcand[:, halves[h]], in_=accs[h][:], func=ACT.Tanh)
+            nc.vector.tensor_tensor(out=ic[:, halves[h]], in0=si[:, halves[h]], in1=tcand[:, halves[h]], op=ALU.mult)
+            nc.vector.tensor_tensor(out=c_new[:, halves[h]], in0=fc[:, halves[h]], in1=ic[:, halves[h]], op=ALU.add)
+            nc.scalar.activation(out=th[:, halves[h]], in_=c_new[:, halves[h]], func=ACT.Tanh)
+        nc.sync.dma_start(out=out_state[:, H:2 * H], in_=c_new[:])
+
+        quarters = [slice(256 * j, 256 * (j + 1)) for j in range(4)]
+        acc_o = [psum.tile([P, 256], F32, name="acc_o%d" % j, tag="bank") for j in range(4)]
+        for k_pass in range(6):
+            for j in range(4):
+                mx(acc_o[j], "o", k_pass, quarters[j])
+        for j in range(4):
+            mx(acc_o[j], "o", 6, quarters[j], rhs=words[("v0", "o")][:, quarters[j]])
+        for j in range(4):
+            mx(acc_o[j], "o", 7, quarters[j], rhs=words[("v1", j)][:])
+            so = keep.tile([P, 256], F32, name="so%d" % j)
+            h_new = keep.tile([P, 256], F32, name="h_new%d" % j)
+            nc.scalar.activation(out=so[:], in_=acc_o[j][:], func=ACT.Sigmoid)
+            nc.vector.tensor_tensor(out=h_new[:], in0=so[:], in1=th[:, quarters[j]], op=ALU.mult)
+            nc.sync.dma_start(out=out_h[:, quarters[j]], in_=h_new[:])
+            nc.sync.dma_start(out=out_state[:, quarters[j]], in_=h_new[:])

@@ -16,7 +16,7 @@ FLOPS = 2 * 128 * 4096 * 4096
 BYTES = 20185088
 
 GATE_SLOT = {"i": 0, "f": 1, "o": 2, "c": 3}
-SW_SCALES = True
+N_HW_SETS = 4
 
 
 def tile_bilaterallstmcell_w_kernel(tc, x, hm1, hm2, *rest):
@@ -64,13 +64,19 @@ def tile_bilaterallstmcell_w_kernel(tc, x, hm1, hm2, *rest):
                 else:
                     nc.gpsimd.dma_start(out=dst.bitcast(F32), in_=rows.bitcast(F32))
 
-        load_scales("f", "w", True)
-        for gate in "fico":
-            for which in "wuv":
-                if (gate, which) != ("f", "w"):
-                    load_scales(gate, which, not SW_SCALES)
+        scale_sets = [(gate, which) for gate in "fico" for which in "wuv"]
+        for gate, which in scale_sets[N_HW_SETS:]:
+            load_scales(gate, which, False)
+        issued = []
+
+        def next_hw_scales():
+            n = len(issued)
+            if n < N_HW_SETS:
+                issued.append(n)
+                load_scales(scale_sets[n][0], scale_sets[n][1], True)
 
         words = {}
+        next_hw_scales()
         for gate in "fico":
             ins = gate_inputs(gate)
             w_src = ins[0].rearrange("g p n t -> p g (n t)")
@@ -80,10 +86,12 @@ def tile_bilaterallstmcell_w_kernel(tc, x, hm1, hm2, *rest):
                 t = keep.tile([P, 2, H], U32, name="%s_%s" % (name, gate), align_bytes=64)
                 nc.sync.dma_start(out=t[:].bitcast(I32), in_=src.bitcast(I32))
                 words[(name, gate)] = t
+                next_hw_scales()
             if gate != "o":
                 t = keep.tile([P, 2, H], U32, name="v01_%s" % gate, align_bytes=64)
                 nc.sync.dma_start(out=t[:].bitcast(I32), in_=v_src.bitcast(I32))
                 words[("v01", gate)] = t
+                next_hw_scales()
             else:
                 t = keep.tile([P, H], U32, name="v0_o", align_bytes=64)
                 nc.sync.dma_start(out=t[:].bitcast(I32), in_=v_src[:, 0, :].bitcast(I32))

@@ -16,7 +16,7 @@ FLOPS = 2 * 128 * 4096 * 4096
 BYTES = 20185088
 
 GATE_SLOT = {"i": 0, "f": 1, "o": 2, "c": 3}
-N_HW_SETS = 4
+N_HW_SETS = 0
 
 
 def tile_bilaterallstmcell_w_kernel(tc, x, hm1, hm2, *rest):
@@ -82,24 +82,18 @@ def tile_bilaterallstmcell_w_kernel(tc, x, hm1, hm2, *rest):
             w_src = ins[0].rearrange("g p n t -> p g (n t)")
             u_src = ins[2].rearrange("g p n t -> p g (n t)")
             v_src = ins[4].rearrange("g p n t -> p g (n t)")
-            for name, src in (("w01", w_src[:, 0:2, :]), ("w23", w_src[:, 2:4, :]), ("u01", u_src)):
-                t = keep.tile([P, 2, H], U32, name="%s_%s" % (name, gate), align_bytes=64)
+            if gate != "o":
+                pieces = (("w01", w_src[:, 0:2, :], H), ("w23", w_src[:, 2:4, :], H), ("u01", u_src, H), ("v01", v_src, H))
+            else:
+                pieces = (("w01", w_src[:, 0:2, :], H), ("w23", w_src[:, 2:4, :], H),
+                          ("u_a", u_src[:, :, 0:2048], 512), ("v_a", v_src[:, :, 0:2048], 512),
+                          ("u_b", u_src[:, :, 2048:4096], 512),
+                          ("v_c", v_src[:, :, 2048:3072], 256), ("v_d", v_src[:, :, 3072:4096], 256))
+            for name, src, width in pieces:
+                t = keep.tile([P, 2, width], U32, name="%s_%s" % (name, gate), align_bytes=64)
                 nc.sync.dma_start(out=t[:].bitcast(I32), in_=src.bitcast(I32))
                 words[(name, gate)] = t
                 next_hw_scales()
-            if gate != "o":
-                t = keep.tile([P, 2, H], U32, name="v01_%s" % gate, align_bytes=64)
-                nc.sync.dma_start(out=t[:].bitcast(I32), in_=v_src.bitcast(I32))
-                words[("v01", gate)] = t
-                next_hw_scales()
-            else:
-                t = keep.tile([P, H], U32, name="v0_o", align_bytes=64)
-                nc.sync.dma_start(out=t[:].bitcast(I32), in_=v_src[:, 0, :].bitcast(I32))
-                words[("v0", gate)] = t
-                for j in range(4):
-                    t = keep.tile([P, 256], U32, name="v1_o_%d" % j, align_bytes=64)
-                    nc.sync.dma_start(out=t[:].bitcast(I32), in_=v_src[:, 1, 1024 * j:1024 * (j + 1)].bitcast(I32))
-                    words[("v1", j)] = t
 
         sources = (
             (x_sb[:].bitcast(F32), 0), (x_sb[:].bitcast(F32), 2),
@@ -191,18 +185,31 @@ def tile_bilaterallstmcell_w_kernel(tc, x, hm1, hm2, *rest):
             nc.scalar.activation(out=th[:, halves[h]], in_=c_new[:, halves[h]], func=ACT.Tanh)
         nc.sync.dma_start(out=out_state[:, H:2 * H], in_=c_new[:])
 
-        quarters = [slice(256 * j, 256 * (j + 1)) for j in range(4)]
-        acc_o = [psum.tile([P, 256], F32, name="acc_o%d" % j, tag="bank") for j in range(4)]
-        for k_pass in range(6):
-            for j in range(4):
-                mx(acc_o[j], "o", k_pass, quarters[j])
-        for j in range(4):
-            mx(acc_o[j], "o", 6, quarters[j], rhs=words[("v0", "o")][:, quarters[j]])
-        for j in range(4):
-            mx(acc_o[j], "o", 7, quarters[j], rhs=words[("v1", j)][:])
-            so = keep.tile([P, 256], F32, name="so%d" % j)
-            h_new = keep.tile([P, 256], F32, name="h_new%d" % j)
-            nc.scalar.activation(out=so[:], in_=acc_o[j][:], func=ACT.Sigmoid)
-            nc.vector.tensor_tensor(out=h_new[:], in0=so[:], in1=th[:, quarters[j]], op=ALU.mult)
-            nc.sync.dma_start(out=out_h[:, quarters[j]], in_=h_new[:])
-            nc.sync.dma_start(out=out_state[:, quarters[j]], in_=h_new[:])
+        parts = (("a", 0, 512), ("c", 512, 768), ("d", 768, 1024))
+        acc_o = {}
+        for part, lo, hi in parts:
+            acc_o[part] = psum.tile([P, hi - lo], F32, name="acc_o_%s" % part, tag="bank")
+        for k_pass in range(4):
+            for part, lo, hi in parts:
+                mx(acc_o[part], "o", k_pass, slice(lo, hi))
+
+        def finish(part, lo, hi):
+            so = keep.tile([P, hi - lo], F32, name="so_%s" % part)
+            h_new = keep.tile([P, hi - lo], F32, name="h_new_%s" % part)
+            nc.scalar.activation(out=so[:], in_=acc_o[part][:], func=ACT.Sigmoid)
+            nc.vector.tensor_tensor(out=h_new[:], in0=so[:], in1=th[:, lo:hi], op=ALU.mult)
+            nc.sync.dma_start(out=out_h[:, lo:hi], in_=h_new[:])
+            nc.sync.dma_start(out=out_state[:, lo:hi], in_=h_new[:])
+
+        for g in range(2):
+            mx(acc_o["a"], "o", 4 + g, slice(0, 512), rhs=words[("u_a", "o")][:, g, :])
+        for g in range(2):
+            mx(acc_o["a"], "o", 6 + g, slice(0, 512), rhs=words[("v_a", "o")][:, g, :])
+        finish("a", 0, 512)
+        for g in range(2):
+            mx(acc_o["c"], "o", 4 + g, slice(512, 768), rhs=words[("u_b", "o")][:, g, 0:256])
+            mx(acc_o["d"], "o", 4 + g, slice(768, 1024), rhs=words[("u_b", "o")][:, g, 256:512])
+        for part, lo, hi in parts[1:]:
+            for g in range(2):
+                mx(acc_o[part], "o", 6 + g, slice(lo, hi), rhs=words[("v_%s" % part, "o")][:, g, :])
+            finish(part, lo, hi)

@@ -16,7 +16,7 @@ FLOPS = 2 * 128 * 4096 * 4096
 BYTES = 20185088
 
 GATE_SLOT = {"i": 0, "f": 1, "o": 2, "c": 3}
-N_HW_SETS = 0
+N_HW_SETS = 2
 
 
 def tile_bilaterallstmcell_w_kernel(tc, x, hm1, hm2, *rest):
@@ -196,8 +196,9 @@ def tile_bilaterallstmcell_w_kernel(tc, x, hm1, hm2, *rest):
         def finish(part, lo, hi):
             so = keep.tile([P, hi - lo], F32, name="so_%s" % part)
             h_new = keep.tile([P, hi - lo], F32, name="h_new_%s" % part)
-            nc.scalar.activation(out=so[:], in_=acc_o[part][:], func=ACT.Sigmoid)
-            nc.vector.tensor_tensor(out=h_new[:], in0=so[:], in1=th[:, lo:hi], op=ALU.mult)
+            for at in range(0, hi - lo, 256):
+                nc.scalar.activation(out=so[:, at:at + 256], in_=acc_o[part][:, at:at + 256], func=ACT.Sigmoid)
+                nc.vector.tensor_tensor(out=h_new[:, at:at + 256], in0=so[:, at:at + 256], in1=th[:, lo + at:lo + at + 256], op=ALU.mult)
             nc.sync.dma_start(out=out_h[:, lo:hi], in_=h_new[:])
             nc.sync.dma_start(out=out_state[:, lo:hi], in_=h_new[:])
 

@@ -37,7 +37,6 @@ def tile_bilaterallstmcell_w_kernel(tc, x, hm1, hm2, *rest):
         warm = keep.tile([P, 8], F32, name="warm")
         warm2 = keep.tile([P, 8], F32, name="warm2")
         nc.vector.memset(warm[:], 0.0)
-        nc.scalar.activation(out=warm2[:], in_=warm[:], func=ACT.Sigmoid)
         ident = keep.tile([P, P], F32, name="ident")
         make_identity(nc, ident[:])
 
@@ -60,7 +59,7 @@ def tile_bilaterallstmcell_w_kernel(tc, x, hm1, hm2, *rest):
                 dst = pl[32 * q + first:32 * q + first + count, :]
                 rows = src[:, 4 * q:4 * q + 4, :]
                 if hw:
-                    nc.sync.dma_start(out=dst.bitcast(I32), in_=rows.bitcast(I32))
+                    nc.scalar.dma_start(out=dst.bitcast(F32), in_=rows.bitcast(F32))
                 else:
                     nc.gpsimd.dma_start(out=dst.bitcast(F32), in_=rows.bitcast(F32))
 
@@ -77,6 +76,7 @@ def tile_bilaterallstmcell_w_kernel(tc, x, hm1, hm2, *rest):
 
         words = {}
         next_hw_scales()
+        nc.scalar.activation(out=warm2[:], in_=warm[:], func=ACT.Sigmoid)
         for gate in "fico":
             ins = gate_inputs(gate)
             w_src = ins[0].rearrange("g p n t -> p g (n t)")

@@ -16,7 +16,7 @@ FLOPS = 2 * 128 * 4096 * 4096
 BYTES = 20185088
 
 GATE_SLOT = {"i": 0, "f": 1, "o": 2, "c": 3}
-N_HW_SETS = 2
+N_HW_SETS = 1
 
 
 def tile_bilaterallstmcell_w_kernel(tc, x, hm1, hm2, *rest):

@@ -16,7 +16,6 @@ FLOPS = 2 * 128 * 4096 * 4096
 BYTES = 20185088
 
 GATE_SLOT = {"i": 0, "f": 1, "o": 2, "c": 3}
-N_HW_SETS = 1
 
 
 def tile_bilaterallstmcell_w_kernel(tc, x, hm1, hm2, *rest):
@@ -30,7 +29,7 @@ def tile_bilaterallstmcell_w_kernel(tc, x, hm1, hm2, *rest):
     with tc.tile_pool(name="keep", bufs=1) as keep, tc.psum_pool(name="psum", bufs=8) as psum, tc.manual_schedule():
         planes = {}
         for gate in "fico":
-            for kind in ("w", "uv"):
+            for kind in (("w", "u", "v") if gate == "o" else ("w", "uv")):
                 pl = keep.tile([P, H], U8, name="pl_%s_%s" % (kind, gate), align_bytes=64)
                 nc.vector.memset(pl[:].bitcast(I32), 0)
                 planes[(kind, gate)] = pl
@@ -47,15 +46,17 @@ def tile_bilaterallstmcell_w_kernel(tc, x, hm1, hm2, *rest):
         nc.sync.dma_start(out=hm1_sb[:], in_=hm1)
         nc.sync.dma_start(out=hc_sb[:], in_=hm2[:, 0:H])
 
-        def load_scales(gate, which, hw):
+        def load_scales(gate, which, hw, quadrants):
             ins = gate_inputs(gate)
             if which == "w":
                 src, pl, first, count = ins[1], planes[("w", gate)], 0, 16
+            elif gate == "o":
+                src, pl, first, count = ins[3 if which == "u" else 5], planes[(which, gate)], 0, 8
             elif which == "u":
                 src, pl, first, count = ins[3], planes[("uv", gate)], 0, 8
             else:
                 src, pl, first, count = ins[5], planes[("uv", gate)], 8, 8
-            for q in range(4):
+            for q in quadrants:
                 dst = pl[32 * q + first:32 * q + first + count, :]
                 rows = src[:, 4 * q:4 * q + 4, :]
                 if hw:
@@ -64,15 +65,17 @@ def tile_bilaterallstmcell_w_kernel(tc, x, hm1, hm2, *rest):
                     nc.gpsimd.dma_start(out=dst.bitcast(F32), in_=rows.bitcast(F32))
 
         scale_sets = [(gate, which) for gate in "fico" for which in "wuv"]
-        for gate, which in scale_sets[N_HW_SETS:]:
-            load_scales(gate, which, False)
+        for gate, which in scale_sets[1:]:
+            load_scales(gate, which, False, range(3) if (gate, which) == ("o", "v") else range(4))
         issued = []
 
         def next_hw_scales():
             n = len(issued)
-            if n < N_HW_SETS:
-                issued.append(n)
-                load_scales(scale_sets[n][0], scale_sets[n][1], True)
+            issued.append(n)
+            if n == 0:
+                load_scales("f", "w", True, range(4))
+            elif n == 1:
+                load_scales("o", "v", True, range(3, 4))
 
         words = {}
         next_hw_scales()
@@ -149,7 +152,7 @@ def tile_bilaterallstmcell_w_kernel(tc, x, hm1, hm2, *rest):
             if rhs is None:
                 rhs, rhs_scale = moving(gate, k_pass, cols)
             else:
-                rhs_scale = plane_rows(planes[("uv", gate)], 4 * (k_pass - 4), cols)
+                rhs_scale = plane_rows(planes[("u" if k_pass < 6 else "v", gate)], 4 * (k_pass % 2), cols)
             nc.tensor.matmul_mx(out=acc[:], lhsT=lhsT, lhsT_scale=lhsT_scale, rhs=rhs.bitcast(FP8X4), rhs_scale=rhs_scale,
                                 start=(k_pass == 0), stop=(k_pass == 7))
 

import concourse.mybir as mybir
from concourse.masks import make_identity

F32 = mybir.dt.float32
BF16 = mybir.dt.bfloat16
I32 = mybir.dt.int32
U32 = mybir.dt.uint32
U8 = mybir.dt.uint8
FP8X4 = mybir.dt.float8_e4m3fn_x4
ACT = mybir.ActivationFunctionType
ALU = mybir.AluOpType

P = 128
H = 1024
FLOPS = 2 * 128 * 4096 * 4096
BYTES = 20185088

GATE_SLOT = {"i": 0, "f": 1, "o": 2, "c": 3}


def tile_bilaterallstmcell_w_kernel(tc, x, hm1, hm2, *rest):
    nc = tc.nc
    out_h, out_state = rest[24], rest[25]

    def gate_inputs(gate):
        base = 6 * GATE_SLOT[gate]
        return rest[base:base + 6]

    with tc.tile_pool(name="keep", bufs=1) as keep, tc.psum_pool(name="psum", bufs=8) as psum, tc.manual_schedule():
        planes = {}
        for gate in "fico":
            for kind in (("w", "u", "v") if gate == "o" else ("w", "uv")):
                pl = keep.tile([P, H], U8, name="pl_%s_%s" % (kind, gate), align_bytes=64)
                nc.vector.memset(pl[:].bitcast(I32), 0)
                planes[(kind, gate)] = pl
        warm = keep.tile([P, 8], F32, name="warm")
        warm2 = keep.tile([P, 8], F32, name="warm2")
        nc.vector.memset(warm[:], 0.0)
        ident = keep.tile([P, P], F32, name="ident")
        make_identity(nc, ident[:])

        x_sb = keep.tile([P, 2048], BF16, name="x_sb")
        hm1_sb = keep.tile([P, 2048], BF16, name="hm1_sb")
        hc_sb = keep.tile([P, H], BF16, name="hc_sb")
        nc.sync.dma_start(out=x_sb[:], in_=x)
        nc.sync.dma_start(out=hm1_sb[:], in_=hm1)
        nc.sync.dma_start(out=hc_sb[:], in_=hm2[:, 0:H])

        def load_scales(gate, which, hw, quadrants):
            ins = gate_inputs(gate)
            if which == "w":
                src, pl, first, count = ins[1], planes[("w", gate)], 0, 16
            elif gate == "o":
                src, pl, first, count = ins[3 if which == "u" else 5], planes[(which, gate)], 0, 8
            elif which == "u":
                src, pl, first, count = ins[3], planes[("uv", gate)], 0, 8
            else:
                src, pl, first, count = ins[5], planes[("uv", gate)], 8, 8
            for q in quadrants:
                dst = pl[32 * q + first:32 * q + first + count, :]
                rows = src[:, 4 * q:4 * q + 4, :]
                if hw:
                    nc.scalar.dma_start(out=dst.bitcast(F32), in_=rows.bitcast(F32))
                else:
                    nc.gpsimd.dma_start(out=dst.bitcast(F32), in_=rows.bitcast(F32))

        scale_sets = [(gate, which) for gate in "fico" for which in "wuv"]
        for gate, which in scale_sets[1:]:
            load_scales(gate, which, False, range(3) if (gate, which) == ("o", "v") else range(4))
        issued = []

        def next_hw_scales():
            n = len(issued)
            issued.append(n)
            if n == 0:
                load_scales("f", "w", True, range(4))
            elif n == 1:
                load_scales("o", "v", True, range(3, 4))

        words = {}
        next_hw_scales()
        nc.scalar.activation(out=warm2[:], in_=warm[:], func=ACT.Sigmoid)
        for gate in "fico":
            ins = gate_inputs(gate)
            w_src = ins[0].rearrange("g p n t -> p g (n t)")
            u_src = ins[2].rearrange("g p n t -> p g (n t)")
            v_src = ins[4].rearrange("g p n t -> p g (n t)")
            if gate != "o":
                pieces = (("w01", w_src[:, 0:2, :], H), ("w23", w_src[:, 2:4, :], H), ("u01", u_src, H), ("v01", v_src, H))
            else:
                pieces = (("w01", w_src[:, 0:2, :], H), ("w23", w_src[:, 2:4, :], H),
                          ("u_a", u_src[:, :, 0:2048], 512), ("v_a", v_src[:, :, 0:2048], 512),
                          ("u_b", u_src[:, :, 2048:4096], 512),
                          ("v_c", v_src[:, :, 2048:3072], 256), ("v_d", v_src[:, :, 3072:4096], 256))
            for name, src, width in pieces:
                t = keep.tile([P, 2, width], U32, name="%s_%s" % (name, gate), align_bytes=64)
                nc.sync.dma_start(out=t[:].bitcast(I32), in_=src.bitcast(I32))
                words[(name, gate)] = t
                next_hw_scales()

        sources = (
            (x_sb[:].bitcast(F32), 0), (x_sb[:].bitcast(F32), 2),
            (hm1_sb[:].bitcast(F32), 0), (hc_sb[:].bitcast(F32), 0),
        )
        banks = []
        for b, (src, g0) in enumerate(sources):
            xt = psum.tile([P, 512], F32, name="xt%d" % b, tag="bank")
            for gl in range(2):
                for u in range(2):
                    g = g0 + gl
                    nc.tensor.transpose(xt[:, (2 * gl + u) * P:(2 * gl + u + 1) * P], src[:, 256 * g + u:256 * (g + 1):2], ident[:])
            banks.append(xt)
        grouped = []
        for b in (0, 2, 1, 3):
            gr = keep.tile([P, 1024], BF16, name="grouped%d" % b, align_bytes=64)
            dst = gr[:].bitcast(F32).rearrange("p (g b u) -> p g b u", g=2, u=2)
            srcv = banks[b][:].rearrange("p (g u b) -> p g b u", g=2, u=2)
            if b % 2 == 0:
                nc.vector.tensor_copy(out=dst, in_=srcv)
            else:
                nc.scalar.copy(out=dst, in_=srcv)
            grouped.append((b, gr))
        grouped = dict(grouped)
        a_codes, a_scales = [], []
        for b in range(4):
            co = keep.tile([P, 256], U32, name="a_codes%d" % b, align_bytes=64)
            sc = keep.tile([P, 256], U8, name="a_scales%d" % b, align_bytes=64)
            nc.vector.quantize_mx(out=co[:].bitcast(FP8X4), scales=sc[:], in_=grouped[b][:])
            a_codes.append(co)
            a_scales.append(sc)

        def stationary(k_pass):
            b, l = k_pass // 2, k_pass % 2
            return a_codes[b][:, l * P:(l + 1) * P].bitcast(FP8X4), a_scales[b][:, l * P:(l + 1) * P]

        def plane_rows(pl, offset, cols):
            if offset == 0:
                return pl[:, cols]
            return pl[offset:P, cols]

        def moving(gate, k_pass, cols):
            if k_pass < 4:
                t = words[("w01" if k_pass < 2 else "w23", gate)]
                return t[:, k_pass % 2, cols], plane_rows(planes[("w", gate)], 4 * k_pass, cols)
            pl = plane_rows(planes[("uv", gate)], 4 * (k_pass - 4), cols)
            if k_pass < 6:
                return words[("u01", gate)][:, k_pass - 4, cols], pl
            return words[("v01", gate)][:, k_pass - 6, cols], pl

        def mx(acc, gate, k_pass, cols, rhs=None):
            lhsT, lhsT_scale = stationary(k_pass)
            if rhs is None:
                rhs, rhs_scale = moving(gate, k_pass, cols)
            else:
                rhs_scale = plane_rows(planes[("u" if k_pass < 6 else "v", gate)], 4 * (k_pass % 2), cols)
            nc.tensor.matmul_mx(out=acc[:], lhsT=lhsT, lhsT_scale=lhsT_scale, rhs=rhs.bitcast(FP8X4), rhs_scale=rhs_scale,
                                start=(k_pass == 0), stop=(k_pass == 7))

        def gate_sums(gate):
            accs = [psum.tile([P, 512], F32, name="acc_%s%d" % (gate, h), tag="bank") for h in range(2)]
            for k_pass in range(8):
                for h in range(2):
                    mx(accs[h], gate, k_pass, slice(512 * h, 512 * (h + 1)))
            return accs

        halves = [slice(0, 512), slice(512, 1024)]
        c_prev = hm1_sb[:, H:2 * H]
        sf = keep.tile([P, H], F32, name="sf")
        fc = keep.tile([P, H], F32, name="fc")
        si = keep.tile([P, H], F32, name="si")
        tcand = keep.tile([P, H], F32, name="tcand")
        ic = keep.tile([P, H], F32, name="ic")
        c_new = keep.tile([P, H], F32, name="c_new")
        th = keep.tile([P, H], F32, name="th")

        accs = gate_sums("f")
        for h in range(2):
            nc.scalar.activation(out=sf[:, halves[h]], in_=accs[h][:], func=ACT.Sigmoid)
            nc.vector.tensor_tensor(out=fc[:, halves[h]], in0=sf[:, halves[h]], in1=c_prev[:, halves[h]], op=ALU.mult)
        accs = gate_sums("i")
        for h in range(2):
            nc.scalar.activation(out=si[:, halves[h]], in_=accs[h][:], func=ACT.Sigmoid)
        accs = gate_sums("c")
        for h in range(2):
            nc.scalar.activation(out=tcand[:, halves[h]], in_=accs[h][:], func=ACT.Tanh)
            nc.vector.tensor_tensor(out=ic[:, halves[h]], in0=si[:, halves[h]], in1=tcand[:, halves[h]], op=ALU.mult)
            nc.vector.tensor_tensor(out=c_new[:, halves[h]], in0=fc[:, halves[h]], in1=ic[:, halves[h]], op=ALU.add)
            nc.scalar.activation(out=th[:, halves[h]], in_=c_new[:, halves[h]], func=ACT.Tanh)
        nc.sync.dma_start(out=out_state[:, H:2 * H], in_=c_new[:])

        parts = (("a", 0, 512), ("c", 512, 768), ("d", 768, 1024))
        acc_o = {}
        for part, lo, hi in parts:
            acc_o[part] = psum.tile([P, hi - lo], F32, name="acc_o_%s" % part, tag="bank")
        for k_pass in range(4):
            for part, lo, hi in parts:
                mx(acc_o[part], "o", k_pass, slice(lo, hi))

        def finish(part, lo, hi):
            so = keep.tile([P, hi - lo], F32, name="so_%s" % part)
            h_new = keep.tile([P, hi - lo], F32, name="h_new_%s" % part)
            for at in range(0, hi - lo, 256):
                nc.scalar.activation(out=so[:, at:at + 256], in_=acc_o[part][:, at:at + 256], func=ACT.Sigmoid)
                nc.vector.tensor_tensor(out=h_new[:, at:at + 256], in0=so[:, at:at + 256], in1=th[:, lo + at:lo + at + 256], op=ALU.mult)
            nc.sync.dma_start(out=out_h[:, lo:hi], in_=h_new[:])
            nc.sync.dma_start(out=out_state[:, lo:hi], in_=h_new[:])

        for g in range(2):
            mx(acc_o["a"], "o", 4 + g, slice(0, 512), rhs=words[("u_a", "o")][:, g, :])
        for g in range(2):
            mx(acc_o["a"], "o", 6 + g, slice(0, 512), rhs=words[("v_a", "o")][:, g, :])
        finish("a", 0, 512)
        for g in range(2):
            mx(acc_o["c"], "o", 4 + g, slice(512, 768), rhs=words[("u_b", "o")][:, g, 0:256])
            mx(acc_o["d"], "o", 4 + g, slice(768, 1024), rhs=words[("u_b", "o")][:, g, 256:512])
        for part, lo, hi in parts[1:]:
            for g in range(2):
                mx(acc_o[part], "o", 6 + g, slice(lo, hi), rhs=words[("v_%s" % part, "o")][:, g, :])
            finish(part, lo, hi)
